import numpy as np
import ml_dtypes


def mxq(x, axis, fmt="e4m3"):
    dtype, down = {"e4m3": (ml_dtypes.float8_e4m3fn, 7), "e5m2": (ml_dtypes.float8_e5m2, 14)}[fmt]
    v = np.moveaxis(np.asarray(x, np.float32).astype(ml_dtypes.bfloat16).astype(np.float64), axis, -1)
    blocks = v.reshape(v.shape[:-1] + (-1, 32))
    amax = np.abs(blocks).max(-1, keepdims=True)
    byte = np.maximum(np.where(amax > 0, np.frexp(amax)[1] - 1 + 127, 0) - down, 1)
    scale = np.exp2(byte - 127.0)
    codes = (blocks / scale).astype(np.float32).astype(dtype).astype(np.float64)
    return np.moveaxis((codes * scale).reshape(v.shape), -1, axis)


WIDE = False


def mx_kscale(k):
    if not WIDE:
        return np.ones(k)
    levels = np.array([10, -10, 5, -5, 0])
    if k % 512:
        return np.exp2(np.random.permutation(np.resize(levels, k // 32))).repeat(32)
    a = np.empty((k // 512, 16))
    for p in range(k // 512):
        a[p, :8] = np.random.permutation(np.resize(levels, 8))
        for g in range(8):
            far = levels[np.abs(levels - a[p, g]) >= 10]
            a[p, g + 8] = far[np.random.randint(len(far))]
    return np.exp2(a.ravel()).repeat(32)


BF16 = ml_dtypes.bfloat16


def bf(x):
    return np.asarray(x, np.float32).astype(BF16)


def f64(x):
    return np.asarray(x).astype(np.float64)


B, S, DIM, HID, R, NT = 8, 512, 512, 1024, 128, 3
SCALING = 4.0


def lora_out(xa, bw, tw):
    return (xa @ bw) * SCALING * tw[..., None]


def setup_inputs():
    s = mx_kscale(HID)
    return {"h": bf(np.random.standard_normal((B, S, HID)) * 0.7 * s),
            "w2": bf(np.random.standard_normal((HID, DIM)) / np.sqrt(HID) / s[:, None]),
            "ha_down": bf(np.random.standard_normal((B, S, R)) * 0.7),
            "b_down": bf(np.random.standard_normal((R, DIM)) * 0.2 / np.sqrt(R)),
            "tw_down": bf(np.random.uniform(size=(B, S)))}


def reference(h, w2, ha_down, b_down, tw_down):
    base = mxq(f64(h), 2, "e4m3") @ mxq(f64(w2), 0, "e4m3")
    return base + lora_out(f64(ha_down), f64(b_down), f64(tw_down))

@@ -1,0 +1,184 @@
+from contextlib import ExitStack
+
+import concourse.mybir as mybir
+from concourse.masks import make_identity
+
+BF16 = mybir.dt.bfloat16
+F32 = mybir.dt.float32
+U32 = mybir.dt.uint32
+U8 = mybir.dt.uint8
+FP8X4 = mybir.dt.float8_e4m3fn_x4
+MULT = mybir.AluOpType.mult
+ADD = mybir.AluOpType.add
+
+P = 128
+TOKENS = 8 * 512
+HID = 1024
+DIM = 512
+RANK = 128
+SCALING = 4.0
+
+PACK = 4
+K_PASS = P * PACK
+PASSES = HID // K_PASS
+HALVES = 2
+
+TILES = TOKENS // P
+ROUND = 2
+ROUNDS = TILES // ROUND
+HA_CHUNK = 8
+HA_CHUNKS = TILES // HA_CHUNK
+LEAD = HA_CHUNK // ROUND
+BANKS = 4
+
+FLOPS = 2 * TOKENS * HID * DIM + 2 * TOKENS * RANK * DIM
+
+
+def tile_feedforward_pb_t_kernel(tc, h, w2, ha_down, b_down, tw_down, out):
+    nc = tc.nc
+    h_view = h.flatten_outer_dims().rearrange("(p t) k -> p t k", t=TILES)
+    ha_view = ha_down.flatten_outer_dims().rearrange("(p t) r -> p t r", t=TILES)
+    tw_view = tw_down.rearrange("b (q t) -> (b q) t", t=TILES)
+    out_view = out.flatten_outer_dims().rearrange("(p t) n -> p t n", t=TILES)
+
+    with ExitStack() as ctx:
+        keep = ctx.enter_context(tc.tile_pool(name="keep", bufs=1))
+        stage = ctx.enter_context(tc.tile_pool(name="stage", bufs=3))
+        psum = ctx.enter_context(tc.psum_pool(name="psum", bufs=BANKS))
+        ctx.enter_context(tc.manual_schedule())
+
+        tw_sb = keep.tile([P, TILES], BF16, name="tw_sb")
+        ha_sb = [keep.tile([P, HA_CHUNK, RANK], BF16, name="ha%d" % c) for c in range(HA_CHUNKS)]
+        b_sb = keep.tile([P, DIM], BF16, name="b_sb")
+        w_raw = keep.tile([P, PASSES, PACK, DIM], BF16, name="w_raw")
+        h_sb = [keep.tile([P, ROUND, HID], BF16, name="h%d" % r) for r in range(ROUNDS)]
+
+        def load_ha(c):
+            nc.sync.dma_start(out=ha_sb[c][:], in_=ha_view[:, c * HA_CHUNK : (c + 1) * HA_CHUNK, :])
+
+        load_ha(0)
+        nc.sync.dma_start(out=b_sb[:], in_=b_down)
+        for g in range(PASSES):
+            nc.sync.dma_start(
+                out=w_raw[:, g], in_=w2[g * K_PASS : (g + 1) * K_PASS, :].rearrange("(q j) n -> q j n", j=PACK)
+            )
+        for c in range(1, HA_CHUNKS):
+            load_ha(c)
+        nc.sync.dma_start(out=tw_sb[:], in_=tw_view)
+        for r in range(ROUNDS):
+            nc.sync.dma_start(out=h_sb[r][:], in_=h_view[:, r * ROUND : (r + 1) * ROUND, :])
+
+        ident_bf16 = keep.tile([P, P], BF16, name="ident_bf16")
+        make_identity(nc, ident_bf16[:])
+        ident_f32 = keep.tile([P, P], F32, name="ident_f32")
+        make_identity(nc, ident_f32[:])
+        gain = keep.tile([P, TILES], F32, name="gain")
+
+        haT_sb = [keep.tile([P, HA_CHUNK, P], BF16, name="haT%d" % c) for c in range(HA_CHUNKS)]
+        out_sb = [keep.tile([P, ROUND, DIM], F32, name="out%d" % r) for r in range(ROUNDS)]
+
+        def transpose_ha(c):
+            haT_ps = psum.tile([P, HA_CHUNK, P], BF16, tag="transposed")
+            for j in range(HA_CHUNK):
+                nc.tensor.transpose(haT_ps[:, j, :], ha_sb[c][:, j, :], ident_bf16[:])
+            nc.vector.tensor_copy(out=haT_sb[c][:], in_=haT_ps[:])
+
+        def adapter(r, tiles_of_round):
+            for a in tiles_of_round:
+                t = r * ROUND + a
+                lora_ps = psum.tile([P, DIM], F32, tag="product")
+                nc.tensor.matmul(
+                    lora_ps[:], lhsT=haT_sb[t // HA_CHUNK][:, t % HA_CHUNK, :], rhs=b_sb[:], start=True, stop=True
+                )
+                nc.scalar.copy(out=out_sb[r][:, a, :], in_=lora_ps[:])
+
+        w_grouped = keep.tile([P, PASSES, DIM, PACK], BF16, name="w_grouped", align_bytes=64)
+        w_codes = keep.tile([P, PASSES, DIM], U32, name="w_codes", align_bytes=64)
+        w_scales = keep.tile([P, PASSES, DIM], U8, name="w_scales", align_bytes=64)
+
+        def quantise_w2():
+            for g in range(PASSES):
+                nc.vector.tensor_copy(out=w_grouped[:, g], in_=w_raw[:, g].rearrange("q t n -> q n t"))
+            for g in range(PASSES):
+                nc.vector.quantize_mx(
+                    out=w_codes[:, g, :].bitcast(FP8X4),
+                    scales=w_scales[:, g, :],
+                    in_=w_grouped[:, g].rearrange("q n t -> q (n t)"),
+                )
+
+        def transpose_h(r):
+            h_words = h_sb[r][:].bitcast(F32)
+            h_grouped = stage.tile([P, ROUND, PASSES, P, PACK], BF16, tag="h_grouped", align_bytes=64)
+            for a in range(ROUND):
+                hT_ps = psum.tile([P, PASSES * HALVES, P], F32, tag="transposed")
+                for s in range(PASSES * HALVES):
+                    g, u = divmod(s, HALVES)
+                    words = h_words[:, a, g * HALVES * P + u : (g + 1) * HALVES * P : HALVES]
+                    nc.tensor.transpose(hT_ps[:, s, :], words, ident_f32[:])
+                nc.scalar.copy(
+                    out=h_grouped[:, a].bitcast(F32),
+                    in_=hT_ps[:].rearrange("q (g u) m -> q g m u", u=HALVES),
+                )
+            return h_grouped
+
+        def quantised_tiles():
+            h_codes = stage.tile([P, ROUND, PASSES, P], U32, tag="h_codes", align_bytes=64)
+            h_scales = stage.tile([P, ROUND, PASSES, P], U8, tag="h_scales", align_bytes=64)
+            return h_codes, h_scales
+
+        def quantise_h(h_grouped, h_codes, h_scales, a):
+            nc.vector.quantize_mx(
+                out=h_codes[:, a].rearrange("q g m -> q (g m)").bitcast(FP8X4),
+                scales=h_scales[:, a].rearrange("q g m -> q (g m)"),
+                in_=h_grouped[:, a].rearrange("q g m t -> q (g m t)"),
+            )
+
+        def project(h_codes, h_scales, a):
+            base_ps = psum.tile([P, DIM], F32, tag="product")
+            for g in range(PASSES):
+                nc.tensor.matmul_mx(
+                    out=base_ps[:],
+                    lhsT=h_codes[:, a, g, :].bitcast(FP8X4),
+                    lhsT_scale=h_scales[:, a, g, :],
+                    rhs=w_codes[:, g, :].bitcast(FP8X4),
+                    rhs_scale=w_scales[:, g, :],
+                    start=(g == 0),
+                    stop=(g == PASSES - 1),
+                )
+            return base_ps
+
+        transpose_ha(0)
+        for r in range(LEAD):
+            adapter(r, range(ROUND))
+        quantise_w2()
+        for c in range(1, HA_CHUNKS):
+            transpose_ha(c)
+        nc.vector.tensor_scalar_mul(out=gain[:], in0=tw_sb[:], scalar1=SCALING)
+        h_grouped = transpose_h(0)
+        ahead = quantised_tiles()
+        for a in range(ROUND):
+            quantise_h(h_grouped, ahead[0], ahead[1], a)
+
+        for r in range(ROUNDS):
+            h_codes, h_scales = ahead
+            if r + 1 < ROUNDS:
+                h_grouped = transpose_h(r + 1)
+                ahead = quantised_tiles()
+            if r + LEAD < ROUNDS:
+                adapter(r + LEAD, range(0, ROUND // 2))
+            for a in range(ROUND):
+                t = r * ROUND + a
+                base_ps = project(h_codes, h_scales, a)
+                if r + 1 < ROUNDS:
+                    quantise_h(h_grouped, ahead[0], ahead[1], a)
+                nc.vector.scalar_tensor_tensor(
+                    out=out_sb[r][:, a, :],
+                    in0=out_sb[r][:, a, :],
+                    scalar=gain[:, t : t + 1],
+                    in1=base_ps[:],
+                    op0=MULT,
+                    op1=ADD,
+                )
+                nc.sync.dma_start(out=out_view[:, t, :], in_=out_sb[r][:, a, :])
+            if r + LEAD < ROUNDS:
+                adapter(r + LEAD, range(ROUND // 2, ROUND))

@@ -28,8 +28,14 @@ ROUND = 2
 ROUNDS = TILES // ROUND
 HA_CHUNK = 8
 HA_CHUNKS = TILES // HA_CHUNK
-LEAD = HA_CHUNK // ROUND
+CHUNK_ROUNDS = HA_CHUNK // ROUND
+COLUMNS = 4
+H_LEAD = 2
+LEAD = 2
+HA_LEAD = LEAD + 1
 BANKS = 4
+
+WARM_UP = 5
 
 FLOPS = 2 * TOKENS * HID * DIM + 2 * TOKENS * RANK * DIM
 
@@ -56,23 +62,33 @@ def tile_feedforward_pb_t_kernel(tc, h, w2, ha_down, b_down, tw_down, out):
         def load_ha(c):
             nc.sync.dma_start(out=ha_sb[c][:], in_=ha_view[:, c * HA_CHUNK : (c + 1) * HA_CHUNK, :])
 
+        def load_h(r):
+            nc.sync.dma_start(out=h_sb[r][:], in_=h_view[:, r * ROUND : (r + 1) * ROUND, :])
+
         load_ha(0)
         nc.sync.dma_start(out=b_sb[:], in_=b_down)
         for g in range(PASSES):
             nc.sync.dma_start(
                 out=w_raw[:, g], in_=w2[g * K_PASS : (g + 1) * K_PASS, :].rearrange("(q j) n -> q j n", j=PACK)
             )
-        for c in range(1, HA_CHUNKS):
-            load_ha(c)
-        nc.sync.dma_start(out=tw_sb[:], in_=tw_view)
         for r in range(ROUNDS):
-            nc.sync.dma_start(out=h_sb[r][:], in_=h_view[:, r * ROUND : (r + 1) * ROUND, :])
+            load_h(r)
+            if r == 0:
+                nc.sync.dma_start(out=tw_sb[:], in_=tw_view)
+            if r % CHUNK_ROUNDS == 0 and r // CHUNK_ROUNDS + 1 < HA_CHUNKS:
+                load_ha(r // CHUNK_ROUNDS + 1)
 
         ident_bf16 = keep.tile([P, P], BF16, name="ident_bf16")
         make_identity(nc, ident_bf16[:])
         ident_f32 = keep.tile([P, P], F32, name="ident_f32")
         make_identity(nc, ident_f32[:])
         gain = keep.tile([P, TILES], F32, name="gain")
+
+        zeros = keep.tile([P, DIM], BF16, name="zeros")
+        nc.vector.memset(zeros[:], 0.0)
+        for i in range(WARM_UP):
+            warm_ps = psum.tile([P, DIM], F32, tag="product")
+            nc.tensor.matmul(warm_ps[:], lhsT=zeros[:, 0:P], rhs=zeros[:], start=True, stop=True)
 
         haT_sb = [keep.tile([P, HA_CHUNK, P], BF16, name="haT%d" % c) for c in range(HA_CHUNKS)]
         out_sb = [keep.tile([P, ROUND, DIM], F32, name="out%d" % r) for r in range(ROUNDS)]
@@ -98,7 +114,10 @@ def tile_feedforward_pb_t_kernel(tc, h, w2, ha_down, b_down, tw_down, out):
 
         def quantise_w2():
             for g in range(PASSES):
-                nc.vector.tensor_copy(out=w_grouped[:, g], in_=w_raw[:, g].rearrange("q t n -> q n t"))
+                nc.vector.tensor_copy(
+                    out=w_grouped[:, g].rearrange("q (c i) t -> q c t i", i=COLUMNS),
+                    in_=w_raw[:, g].rearrange("q t (c i) -> q c t i", i=COLUMNS),
+                )
             for g in range(PASSES):
                 nc.vector.quantize_mx(
                     out=w_codes[:, g, :].bitcast(FP8X4),
@@ -126,11 +145,11 @@ def tile_feedforward_pb_t_kernel(tc, h, w2, ha_down, b_down, tw_down, out):
             h_scales = stage.tile([P, ROUND, PASSES, P], U8, tag="h_scales", align_bytes=64)
             return h_codes, h_scales
 
-        def quantise_h(h_grouped, h_codes, h_scales, a):
+        def quantise_h(h_grouped, h_codes, h_scales):
             nc.vector.quantize_mx(
-                out=h_codes[:, a].rearrange("q g m -> q (g m)").bitcast(FP8X4),
-                scales=h_scales[:, a].rearrange("q g m -> q (g m)"),
-                in_=h_grouped[:, a].rearrange("q g m t -> q (g m t)"),
+                out=h_codes[:].rearrange("q a g m -> q (a g m)").bitcast(FP8X4),
+                scales=h_scales[:].rearrange("q a g m -> q (a g m)"),
+                in_=h_grouped[:].rearrange("q a g m t -> q (a g m t)"),
             )
 
         def project(h_codes, h_scales, a):
@@ -148,29 +167,28 @@ def tile_feedforward_pb_t_kernel(tc, h, w2, ha_down, b_down, tw_down, out):
             return base_ps
 
         transpose_ha(0)
+        h_grouped = {}
         for r in range(LEAD):
             adapter(r, range(ROUND))
         quantise_w2()
-        for c in range(1, HA_CHUNKS):
-            transpose_ha(c)
         nc.vector.tensor_scalar_mul(out=gain[:], in0=tw_sb[:], scalar1=SCALING)
-        h_grouped = transpose_h(0)
-        ahead = quantised_tiles()
-        for a in range(ROUND):
-            quantise_h(h_grouped, ahead[0], ahead[1], a)
+        for r in range(H_LEAD):
+            h_grouped[r] = transpose_h(r)
+        quantised = [quantised_tiles()]
+        quantise_h(h_grouped[0], *quantised[0])
 
         for r in range(ROUNDS):
-            h_codes, h_scales = ahead
+            h_codes, h_scales = quantised[r]
+            if r + H_LEAD < ROUNDS:
+                h_grouped[r + H_LEAD] = transpose_h(r + H_LEAD)
             if r + 1 < ROUNDS:
-                h_grouped = transpose_h(r + 1)
-                ahead = quantised_tiles()
+                quantised.append(quantised_tiles())
+                quantise_h(h_grouped[r + 1], *quantised[r + 1])
             if r + LEAD < ROUNDS:
                 adapter(r + LEAD, range(0, ROUND // 2))
             for a in range(ROUND):
                 t = r * ROUND + a
                 base_ps = project(h_codes, h_scales, a)
-                if r + 1 < ROUNDS:
-                    quantise_h(h_grouped, ahead[0], ahead[1], a)
                 nc.vector.scalar_tensor_tensor(
                     out=out_sb[r][:, a, :],
                     in0=out_sb[r][:, a, :],
@@ -182,3 +200,5 @@ def tile_feedforward_pb_t_kernel(tc, h, w2, ha_down, b_down, tw_down, out):
                 nc.sync.dma_start(out=out_view[:, t, :], in_=out_sb[r][:, a, :])
             if r + LEAD < ROUNDS:
                 adapter(r + LEAD, range(ROUND // 2, ROUND))
+            if (r + HA_LEAD) % CHUNK_ROUNDS == 0 and r + HA_LEAD < ROUNDS:
+                transpose_ha((r + HA_LEAD) // CHUNK_ROUNDS)

@@ -28,6 +28,8 @@ ROUND = 2
 ROUNDS = TILES // ROUND
 HA_CHUNK = 8
 HA_CHUNKS = TILES // HA_CHUNK
+DEALT = 1
+DEAL_AHEAD = 2
 CHUNK_ROUNDS = HA_CHUNK // ROUND
 COLUMNS = 4
 H_LEAD = 2
@@ -125,14 +127,25 @@ def tile_feedforward_pb_t_kernel(tc, h, w2, ha_down, b_down, tw_down, out):
                     in_=w_grouped[:, g].rearrange("q n t -> q (n t)"),
                 )
 
-        def transpose_h(r):
+        def deal_words(r):
+            words = stage.tile([P, PASSES * HALVES * P], F32, tag="dealt", bufs=DEAL_AHEAD + 1)
+            nc.vector.tensor_copy(
+                out=words[:].rearrange("p (g u q) -> p g u q", g=PASSES, u=HALVES),
+                in_=h_sb[r][:, DEALT].bitcast(F32).rearrange("p (g q u) -> p g u q", u=HALVES, q=P),
+            )
+            return words
+
+        def transpose_h(r, dealt=None):
             h_words = h_sb[r][:].bitcast(F32)
             h_grouped = stage.tile([P, ROUND, PASSES, P, PACK], BF16, tag="h_grouped", align_bytes=64)
             for a in range(ROUND):
                 hT_ps = psum.tile([P, PASSES * HALVES, P], F32, tag="transposed")
                 for s in range(PASSES * HALVES):
                     g, u = divmod(s, HALVES)
-                    words = h_words[:, a, g * HALVES * P + u : (g + 1) * HALVES * P : HALVES]
+                    if dealt is not None and a == DEALT:
+                        words = dealt[:, s * P : (s + 1) * P]
+                    else:
+                        words = h_words[:, a, g * HALVES * P + u : (g + 1) * HALVES * P : HALVES]
                     nc.tensor.transpose(hT_ps[:, s, :], words, ident_f32[:])
                 nc.scalar.copy(
                     out=h_grouped[:, a].bitcast(F32),
@@ -171,16 +184,21 @@ def tile_feedforward_pb_t_kernel(tc, h, w2, ha_down, b_down, tw_down, out):
         for r in range(LEAD):
             adapter(r, range(ROUND))
         quantise_w2()
+        h_grouped[0] = transpose_h(0)
+        transpose_ha(1)
         nc.vector.tensor_scalar_mul(out=gain[:], in0=tw_sb[:], scalar1=SCALING)
-        for r in range(H_LEAD):
+        for r in range(1, H_LEAD):
             h_grouped[r] = transpose_h(r)
         quantised = [quantised_tiles()]
         quantise_h(h_grouped[0], *quantised[0])
+        dealt = {r: deal_words(r) for r in range(H_LEAD, H_LEAD + DEAL_AHEAD)}
 
         for r in range(ROUNDS):
             h_codes, h_scales = quantised[r]
             if r + H_LEAD < ROUNDS:
-                h_grouped[r + H_LEAD] = transpose_h(r + H_LEAD)
+                h_grouped[r + H_LEAD] = transpose_h(r + H_LEAD, dealt[r + H_LEAD])
+            if (r + HA_LEAD) % CHUNK_ROUNDS == 0 and CHUNK_ROUNDS < r + HA_LEAD < ROUNDS:
+                transpose_ha((r + HA_LEAD) // CHUNK_ROUNDS)
             if r + 1 < ROUNDS:
                 quantised.append(quantised_tiles())
                 quantise_h(h_grouped[r + 1], *quantised[r + 1])
@@ -198,7 +216,7 @@ def tile_feedforward_pb_t_kernel(tc, h, w2, ha_down, b_down, tw_down, out):
                     op1=ADD,
                 )
                 nc.sync.dma_start(out=out_view[:, t, :], in_=out_sb[r][:, a, :])
+            if r + H_LEAD + DEAL_AHEAD < ROUNDS:
+                dealt[r + H_LEAD + DEAL_AHEAD] = deal_words(r + H_LEAD + DEAL_AHEAD)
             if r + LEAD < ROUNDS:
                 adapter(r + LEAD, range(ROUND // 2, ROUND))
-            if (r + HA_LEAD) % CHUNK_ROUNDS == 0 and r + HA_LEAD < ROUNDS:
-                transpose_ha((r + HA_LEAD) // CHUNK_ROUNDS)

@@ -28,7 +28,7 @@ ROUND = 2
 ROUNDS = TILES // ROUND
 HA_CHUNK = 8
 HA_CHUNKS = TILES // HA_CHUNK
-DEALT = 1
+DEALT = ((0, 1), (1,))
 DEAL_AHEAD = 2
 CHUNK_ROUNDS = HA_CHUNK // ROUND
 COLUMNS = 4
@@ -37,7 +37,7 @@ LEAD = 2
 HA_LEAD = LEAD + 1
 BANKS = 4
 
-WARM_UP = 5
+WARM_UP = 3
 
 FLOPS = 2 * TOKENS * HID * DIM + 2 * TOKENS * RANK * DIM
 
@@ -75,9 +75,9 @@ def tile_feedforward_pb_t_kernel(tc, h, w2, ha_down, b_down, tw_down, out):
             )
         for r in range(ROUNDS):
             load_h(r)
-            if r == 0:
+            if r == H_LEAD:
                 nc.sync.dma_start(out=tw_sb[:], in_=tw_view)
-            if r % CHUNK_ROUNDS == 0 and r // CHUNK_ROUNDS + 1 < HA_CHUNKS:
+            if r % CHUNK_ROUNDS == H_LEAD and r // CHUNK_ROUNDS + 1 < HA_CHUNKS:
                 load_ha(r // CHUNK_ROUNDS + 1)
 
         ident_bf16 = keep.tile([P, P], BF16, name="ident_bf16")
@@ -99,6 +99,9 @@ def tile_feedforward_pb_t_kernel(tc, h, w2, ha_down, b_down, tw_down, out):
             haT_ps = psum.tile([P, HA_CHUNK, P], BF16, tag="transposed")
             for j in range(HA_CHUNK):
                 nc.tensor.transpose(haT_ps[:, j, :], ha_sb[c][:, j, :], ident_bf16[:])
+            return haT_ps
+
+        def copy_ha(c, haT_ps):
             nc.vector.tensor_copy(out=haT_sb[c][:], in_=haT_ps[:])
 
         def adapter(r, tiles_of_round):
@@ -128,22 +131,25 @@ def tile_feedforward_pb_t_kernel(tc, h, w2, ha_down, b_down, tw_down, out):
                 )
 
         def deal_words(r):
-            words = stage.tile([P, PASSES * HALVES * P], F32, tag="dealt", bufs=DEAL_AHEAD + 1)
-            nc.vector.tensor_copy(
-                out=words[:].rearrange("p (g u q) -> p g u q", g=PASSES, u=HALVES),
-                in_=h_sb[r][:, DEALT].bitcast(F32).rearrange("p (g q u) -> p g u q", u=HALVES, q=P),
-            )
-            return words
+            dealt = {}
+            for a in DEALT[r % 2]:
+                words = stage.tile([P, PASSES * HALVES * P], F32, tag="dealt", bufs=2 * (DEAL_AHEAD + 1))
+                nc.vector.tensor_copy(
+                    out=words[:].rearrange("p (g u q) -> p g u q", g=PASSES, u=HALVES),
+                    in_=h_sb[r][:, a].bitcast(F32).rearrange("p (g q u) -> p g u q", u=HALVES, q=P),
+                )
+                dealt[a] = words
+            return dealt
 
-        def transpose_h(r, dealt=None):
+        def transpose_h(r, dealt):
             h_words = h_sb[r][:].bitcast(F32)
             h_grouped = stage.tile([P, ROUND, PASSES, P, PACK], BF16, tag="h_grouped", align_bytes=64)
             for a in range(ROUND):
                 hT_ps = psum.tile([P, PASSES * HALVES, P], F32, tag="transposed")
                 for s in range(PASSES * HALVES):
                     g, u = divmod(s, HALVES)
-                    if dealt is not None and a == DEALT:
-                        words = dealt[:, s * P : (s + 1) * P]
+                    if a in dealt:
+                        words = dealt[a][:, s * P : (s + 1) * P]
                     else:
                         words = h_words[:, a, g * HALVES * P + u : (g + 1) * HALVES * P : HALVES]
                     nc.tensor.transpose(hT_ps[:, s, :], words, ident_f32[:])
@@ -165,57 +171,60 @@ def tile_feedforward_pb_t_kernel(tc, h, w2, ha_down, b_down, tw_down, out):
                 in_=h_grouped[:].rearrange("q a g m t -> q (a g m t)"),
             )
 
-        def project(h_codes, h_scales, a):
-            base_ps = psum.tile([P, DIM], F32, tag="product")
+        def project(h_codes, h_scales, a, cols):
+            base_ps = psum.tile([P, cols.stop - cols.start], F32, tag="product")
             for g in range(PASSES):
                 nc.tensor.matmul_mx(
                     out=base_ps[:],
                     lhsT=h_codes[:, a, g, :].bitcast(FP8X4),
                     lhsT_scale=h_scales[:, a, g, :],
-                    rhs=w_codes[:, g, :].bitcast(FP8X4),
-                    rhs_scale=w_scales[:, g, :],
+                    rhs=w_codes[:, g, cols].bitcast(FP8X4),
+                    rhs_scale=w_scales[:, g, cols],
                     start=(g == 0),
                     stop=(g == PASSES - 1),
                 )
             return base_ps
 
-        transpose_ha(0)
+        copy_ha(0, transpose_ha(0))
         h_grouped = {}
         for r in range(LEAD):
             adapter(r, range(ROUND))
         quantise_w2()
-        h_grouped[0] = transpose_h(0)
-        transpose_ha(1)
-        nc.vector.tensor_scalar_mul(out=gain[:], in0=tw_sb[:], scalar1=SCALING)
-        for r in range(1, H_LEAD):
-            h_grouped[r] = transpose_h(r)
+        for r in range(H_LEAD):
+            h_grouped[r] = transpose_h(r, {})
         quantised = [quantised_tiles()]
         quantise_h(h_grouped[0], *quantised[0])
-        dealt = {r: deal_words(r) for r in range(H_LEAD, H_LEAD + DEAL_AHEAD)}
+        nc.vector.tensor_scalar_mul(out=gain[:], in0=tw_sb[:], scalar1=SCALING)
+        dealt = {}
 
         for r in range(ROUNDS):
             h_codes, h_scales = quantised[r]
             if r + H_LEAD < ROUNDS:
-                h_grouped[r + H_LEAD] = transpose_h(r + H_LEAD, dealt[r + H_LEAD])
-            if (r + HA_LEAD) % CHUNK_ROUNDS == 0 and CHUNK_ROUNDS < r + HA_LEAD < ROUNDS:
-                transpose_ha((r + HA_LEAD) // CHUNK_ROUNDS)
+                h_grouped[r + H_LEAD] = transpose_h(r + H_LEAD, dealt.get(r + H_LEAD, {}))
+            c, rest = divmod(r + HA_LEAD, CHUNK_ROUNDS)
+            haT_ps = transpose_ha(c) if rest == 0 and c < HA_CHUNKS else None
             if r + 1 < ROUNDS:
                 quantised.append(quantised_tiles())
                 quantise_h(h_grouped[r + 1], *quantised[r + 1])
+            if haT_ps is not None:
+                copy_ha(c, haT_ps)
             if r + LEAD < ROUNDS:
                 adapter(r + LEAD, range(0, ROUND // 2))
             for a in range(ROUND):
                 t = r * ROUND + a
-                base_ps = project(h_codes, h_scales, a)
-                nc.vector.scalar_tensor_tensor(
-                    out=out_sb[r][:, a, :],
-                    in0=out_sb[r][:, a, :],
-                    scalar=gain[:, t : t + 1],
-                    in1=base_ps[:],
-                    op0=MULT,
-                    op1=ADD,
-                )
-                nc.sync.dma_start(out=out_view[:, t, :], in_=out_sb[r][:, a, :])
+                width = DIM // 2 if t == TILES - 1 else DIM
+                for n in range(0, DIM, width):
+                    cols = slice(n, n + width)
+                    base_ps = project(h_codes, h_scales, a, cols)
+                    nc.vector.scalar_tensor_tensor(
+                        out=out_sb[r][:, a, cols],
+                        in0=out_sb[r][:, a, cols],
+                        scalar=gain[:, t : t + 1],
+                        in1=base_ps[:],
+                        op0=MULT,
+                        op1=ADD,
+                    )
+                    nc.sync.dma_start(out=out_view[:, t, cols], in_=out_sb[r][:, a, cols])
             if r + H_LEAD + DEAL_AHEAD < ROUNDS:
                 dealt[r + H_LEAD + DEAL_AHEAD] = deal_words(r + H_LEAD + DEAL_AHEAD)
             if r + LEAD < ROUNDS:

from contextlib import ExitStack

import concourse.mybir as mybir
from concourse.masks import make_identity

BF16 = mybir.dt.bfloat16
F32 = mybir.dt.float32
U32 = mybir.dt.uint32
U8 = mybir.dt.uint8
FP8X4 = mybir.dt.float8_e4m3fn_x4
MULT = mybir.AluOpType.mult
ADD = mybir.AluOpType.add

P = 128
TOKENS = 8 * 512
HID = 1024
DIM = 512
RANK = 128
SCALING = 4.0

PACK = 4
K_PASS = P * PACK
PASSES = HID // K_PASS
HALVES = 2

TILES = TOKENS // P
ROUND = 2
ROUNDS = TILES // ROUND
HA_CHUNK = 8
HA_CHUNKS = TILES // HA_CHUNK
DEALT = ((0, 1), (1,))
DEAL_AHEAD = 2
CHUNK_ROUNDS = HA_CHUNK // ROUND
COLUMNS = 4
H_LEAD = 2
LEAD = 2
HA_LEAD = LEAD + 1
BANKS = 4

WARM_UP = 3

FLOPS = 2 * TOKENS * HID * DIM + 2 * TOKENS * RANK * DIM


def tile_feedforward_pb_t_kernel(tc, h, w2, ha_down, b_down, tw_down, out):
    nc = tc.nc
    h_view = h.flatten_outer_dims().rearrange("(p t) k -> p t k", t=TILES)
    ha_view = ha_down.flatten_outer_dims().rearrange("(p t) r -> p t r", t=TILES)
    tw_view = tw_down.rearrange("b (q t) -> (b q) t", t=TILES)
    out_view = out.flatten_outer_dims().rearrange("(p t) n -> p t n", t=TILES)

    with ExitStack() as ctx:
        keep = ctx.enter_context(tc.tile_pool(name="keep", bufs=1))
        stage = ctx.enter_context(tc.tile_pool(name="stage", bufs=3))
        psum = ctx.enter_context(tc.psum_pool(name="psum", bufs=BANKS))
        ctx.enter_context(tc.manual_schedule())

        tw_sb = keep.tile([P, TILES], BF16, name="tw_sb")
        ha_sb = [keep.tile([P, HA_CHUNK, RANK], BF16, name="ha%d" % c) for c in range(HA_CHUNKS)]
        b_sb = keep.tile([P, DIM], BF16, name="b_sb")
        w_raw = keep.tile([P, PASSES, PACK, DIM], BF16, name="w_raw")
        h_sb = [keep.tile([P, ROUND, HID], BF16, name="h%d" % r) for r in range(ROUNDS)]

        def load_ha(c):
            nc.sync.dma_start(out=ha_sb[c][:], in_=ha_view[:, c * HA_CHUNK : (c + 1) * HA_CHUNK, :])

        def load_h(r):
            nc.sync.dma_start(out=h_sb[r][:], in_=h_view[:, r * ROUND : (r + 1) * ROUND, :])

        load_ha(0)
        nc.sync.dma_start(out=b_sb[:], in_=b_down)
        for g in range(PASSES):
            nc.sync.dma_start(
                out=w_raw[:, g], in_=w2[g * K_PASS : (g + 1) * K_PASS, :].rearrange("(q j) n -> q j n", j=PACK)
            )
        for r in range(ROUNDS):
            load_h(r)
            if r == H_LEAD:
                nc.sync.dma_start(out=tw_sb[:], in_=tw_view)
            if r % CHUNK_ROUNDS == H_LEAD and r // CHUNK_ROUNDS + 1 < HA_CHUNKS:
                load_ha(r // CHUNK_ROUNDS + 1)

        ident_bf16 = keep.tile([P, P], BF16, name="ident_bf16")
        make_identity(nc, ident_bf16[:])
        ident_f32 = keep.tile([P, P], F32, name="ident_f32")
        make_identity(nc, ident_f32[:])
        gain = keep.tile([P, TILES], F32, name="gain")

        zeros = keep.tile([P, DIM], BF16, name="zeros")
        nc.vector.memset(zeros[:], 0.0)
        for i in range(WARM_UP):
            warm_ps = psum.tile([P, DIM], F32, tag="product")
            nc.tensor.matmul(warm_ps[:], lhsT=zeros[:, 0:P], rhs=zeros[:], start=True, stop=True)

        haT_sb = [keep.tile([P, HA_CHUNK, P], BF16, name="haT%d" % c) for c in range(HA_CHUNKS)]
        out_sb = [keep.tile([P, ROUND, DIM], F32, name="out%d" % r) for r in range(ROUNDS)]

        def transpose_ha(c):
            haT_ps = psum.tile([P, HA_CHUNK, P], BF16, tag="transposed")
            for j in range(HA_CHUNK):
                nc.tensor.transpose(haT_ps[:, j, :], ha_sb[c][:, j, :], ident_bf16[:])
            return haT_ps

        def copy_ha(c, haT_ps):
            nc.vector.tensor_copy(out=haT_sb[c][:], in_=haT_ps[:])

        def adapter(r, tiles_of_round):
            for a in tiles_of_round:
                t = r * ROUND + a
                lora_ps = psum.tile([P, DIM], F32, tag="product")
                nc.tensor.matmul(
                    lora_ps[:], lhsT=haT_sb[t // HA_CHUNK][:, t % HA_CHUNK, :], rhs=b_sb[:], start=True, stop=True
                )
                nc.scalar.copy(out=out_sb[r][:, a, :], in_=lora_ps[:])

        w_grouped = keep.tile([P, PASSES, DIM, PACK], BF16, name="w_grouped", align_bytes=64)
        w_codes = keep.tile([P, PASSES, DIM], U32, name="w_codes", align_bytes=64)
        w_scales = keep.tile([P, PASSES, DIM], U8, name="w_scales", align_bytes=64)

        def quantise_w2():
            for g in range(PASSES):
                nc.vector.tensor_copy(
                    out=w_grouped[:, g].rearrange("q (c i) t -> q c t i", i=COLUMNS),
                    in_=w_raw[:, g].rearrange("q t (c i) -> q c t i", i=COLUMNS),
                )
            for g in range(PASSES):
                nc.vector.quantize_mx(
                    out=w_codes[:, g, :].bitcast(FP8X4),
                    scales=w_scales[:, g, :],
                    in_=w_grouped[:, g].rearrange("q n t -> q (n t)"),
                )

        def deal_words(r):
            dealt = {}
            for a in DEALT[r % 2]:
                words = stage.tile([P, PASSES * HALVES * P], F32, tag="dealt", bufs=2 * (DEAL_AHEAD + 1))
                nc.vector.tensor_copy(
                    out=words[:].rearrange("p (g u q) -> p g u q", g=PASSES, u=HALVES),
                    in_=h_sb[r][:, a].bitcast(F32).rearrange("p (g q u) -> p g u q", u=HALVES, q=P),
                )
                dealt[a] = words
            return dealt

        def transpose_h(r, dealt):
            h_words = h_sb[r][:].bitcast(F32)
            h_grouped = stage.tile([P, ROUND, PASSES, P, PACK], BF16, tag="h_grouped", align_bytes=64)
            for a in range(ROUND):
                hT_ps = psum.tile([P, PASSES * HALVES, P], F32, tag="transposed")
                for s in range(PASSES * HALVES):
                    g, u = divmod(s, HALVES)
                    if a in dealt:
                        words = dealt[a][:, s * P : (s + 1) * P]
                    else:
                        words = h_words[:, a, g * HALVES * P + u : (g + 1) * HALVES * P : HALVES]
                    nc.tensor.transpose(hT_ps[:, s, :], words, ident_f32[:])
                nc.scalar.copy(
                    out=h_grouped[:, a].bitcast(F32),
                    in_=hT_ps[:].rearrange("q (g u) m -> q g m u", u=HALVES),
                )
            return h_grouped

        def quantised_tiles():
            h_codes = stage.tile([P, ROUND, PASSES, P], U32, tag="h_codes", align_bytes=64)
            h_scales = stage.tile([P, ROUND, PASSES, P], U8, tag="h_scales", align_bytes=64)
            return h_codes, h_scales

        def quantise_h(h_grouped, h_codes, h_scales):
            nc.vector.quantize_mx(
                out=h_codes[:].rearrange("q a g m -> q (a g m)").bitcast(FP8X4),
                scales=h_scales[:].rearrange("q a g m -> q (a g m)"),
                in_=h_grouped[:].rearrange("q a g m t -> q (a g m t)"),
            )

        def project(h_codes, h_scales, a, cols):
            base_ps = psum.tile([P, cols.stop - cols.start], F32, tag="product")
            for g in range(PASSES):
                nc.tensor.matmul_mx(
                    out=base_ps[:],
                    lhsT=h_codes[:, a, g, :].bitcast(FP8X4),
                    lhsT_scale=h_scales[:, a, g, :],
                    rhs=w_codes[:, g, cols].bitcast(FP8X4),
                    rhs_scale=w_scales[:, g, cols],
                    start=(g == 0),
                    stop=(g == PASSES - 1),
                )
            return base_ps

        copy_ha(0, transpose_ha(0))
        h_grouped = {}
        for r in range(LEAD):
            adapter(r, range(ROUND))
        quantise_w2()
        for r in range(H_LEAD):
            h_grouped[r] = transpose_h(r, {})
        quantised = [quantised_tiles()]
        quantise_h(h_grouped[0], *quantised[0])
        nc.vector.tensor_scalar_mul(out=gain[:], in0=tw_sb[:], scalar1=SCALING)
        dealt = {}

        for r in range(ROUNDS):
            h_codes, h_scales = quantised[r]
            if r + H_LEAD < ROUNDS:
                h_grouped[r + H_LEAD] = transpose_h(r + H_LEAD, dealt.get(r + H_LEAD, {}))
            c, rest = divmod(r + HA_LEAD, CHUNK_ROUNDS)
            haT_ps = transpose_ha(c) if rest == 0 and c < HA_CHUNKS else None
            if r + 1 < ROUNDS:
                quantised.append(quantised_tiles())
                quantise_h(h_grouped[r + 1], *quantised[r + 1])
            if haT_ps is not None:
                copy_ha(c, haT_ps)
            if r + LEAD < ROUNDS:
                adapter(r + LEAD, range(0, ROUND // 2))
            for a in range(ROUND):
                t = r * ROUND + a
                width = DIM // 2 if t == TILES - 1 else DIM
                for n in range(0, DIM, width):
                    cols = slice(n, n + width)
                    base_ps = project(h_codes, h_scales, a, cols)
                    nc.vector.scalar_tensor_tensor(
                        out=out_sb[r][:, a, cols],
                        in0=out_sb[r][:, a, cols],
                        scalar=gain[:, t : t + 1],
                        in1=base_ps[:],
                        op0=MULT,
                        op1=ADD,
                    )
                    nc.sync.dma_start(out=out_view[:, t, cols], in_=out_sb[r][:, a, cols])
            if r + H_LEAD + DEAL_AHEAD < ROUNDS:
                dealt[r + H_LEAD + DEAL_AHEAD] = deal_words(r + H_LEAD + DEAL_AHEAD)
            if r + LEAD < ROUNDS:
                adapter(r + LEAD, range(ROUND // 2, ROUND))
